import numpy as np
import ml_dtypes


def mxq(x, axis, fmt="e4m3"):
    dtype, down = {"e4m3": (ml_dtypes.float8_e4m3fn, 7), "e5m2": (ml_dtypes.float8_e5m2, 14)}[fmt]
    v = np.moveaxis(np.asarray(x, np.float32).astype(ml_dtypes.bfloat16).astype(np.float64), axis, -1)
    blocks = v.reshape(v.shape[:-1] + (-1, 32))
    amax = np.abs(blocks).max(-1, keepdims=True)
    byte = np.maximum(np.where(amax > 0, np.frexp(amax)[1] - 1 + 127, 0) - down, 1)
    scale = np.exp2(byte - 127.0)
    codes = (blocks / scale).astype(np.float32).astype(dtype).astype(np.float64)
    return np.moveaxis((codes * scale).reshape(v.shape), -1, axis)


WIDE = False


def mx_kscale(k):
    if not WIDE:
        return np.ones(k)
    levels = np.array([10, -10, 5, -5, 0])
    a = np.random.permutation(np.resize(levels, k // 512 * 4)).reshape(k // 512, 4)
    idx = np.arange(k)
    return np.exp2(a[idx // 512, idx % 128 // 32])


BF16 = ml_dtypes.bfloat16


def bf(x):
    return np.asarray(x, np.float32).astype(BF16)


def f64(x):
    return np.asarray(x).astype(np.float64)


B, S, H, D, QB, DEPTH = 1, 1024, 4, 128, 512, 12
HP = H // 2
LAMBDA_INIT = 0.8 - 0.6 * np.exp(-0.3 * DEPTH)
NEG_INF = -1e30
EPS = 1e-5


def split_heads(x):
    x = x.reshape(x.shape[0], x.shape[1], x.shape[2] // 2, 2, x.shape[3])
    return x[..., 0, :], x[..., 1, :]


def causal_attn(q, k, vq):
    rows = []
    for r0 in range(0, S, QB):
        r1 = r0 + QB
        s = (q[:, :, r0:r1] @ k[:, :, :r1].transpose(0, 1, 3, 2)) * (1.0 / np.sqrt(D))
        causal = np.arange(r0, r1)[:, None] >= np.arange(r1)[None, :]
        s = np.where(causal, s, NEG_INF)
        e = np.exp(s - s.max(-1, keepdims=True))
        rows.append((mxq(e, 3, "e4m3") @ vq[:, :, :r1]) / e.sum(-1, keepdims=True))
    return np.concatenate(rows, axis=2)


def setup_inputs():
    ls = 0.5 / D ** 0.25
    t = mx_kscale(S)
    qc = 0.25 * np.sqrt(D)
    q = np.random.standard_normal((B, S, H, D))
    k = np.random.standard_normal((B, S, H, D))
    v = np.random.standard_normal((B, S, H, D)) * 0.125
    q[..., 0] = qc
    k[..., 0] += (np.log(t) * np.sqrt(D) / qc)[None, :, None]
    v *= (t.mean() / t)[None, :, None, None]
    return {
        "q": bf(q),
        "k": bf(k),
        "v": bf(v),
        "lambda_q1": bf(np.random.standard_normal(D) * ls),
        "lambda_k1": bf(np.random.standard_normal(D) * ls),
        "lambda_q2": bf(np.random.standard_normal(D) * ls),
        "lambda_k2": bf(np.random.standard_normal(D) * ls),
        "subln_weight": bf(1.0 + 0.1 * np.random.standard_normal(2 * D)),
    }


def reference(q, k, v, lambda_q1, lambda_k1, lambda_q2, lambda_k2, subln_weight):
    q1, q2 = split_heads(f64(q))
    k1, k2 = split_heads(f64(k))
    v1, v2 = split_heads(f64(v))
    v12 = np.concatenate([v1, v2], axis=-1)
    vq = mxq(v12.transpose(0, 2, 1, 3), 2, "e4m3")
    attn1 = causal_attn(q1.transpose(0, 2, 1, 3), k1.transpose(0, 2, 1, 3), vq)
    attn2 = causal_attn(q2.transpose(0, 2, 1, 3), k2.transpose(0, 2, 1, 3), vq)
    lam1 = np.exp(np.sum(f64(lambda_q1) * f64(lambda_k1)))
    lam2 = np.exp(np.sum(f64(lambda_q2) * f64(lambda_k2)))
    lam = lam1 - lam2 + LAMBDA_INIT
    x = attn1 - lam * attn2
    var = np.mean(x * x, axis=-1, keepdims=True)
    xn = f64(subln_weight) * (x / np.sqrt(var + EPS))
    y = xn * (1.0 - LAMBDA_INIT)
    return y.transpose(0, 2, 1, 3).reshape(B, S, H, D)

@@ -1,0 +1,406 @@
+import math
+from contextlib import ExitStack
+
+import concourse.mybir as mybir
+from concourse.masks import make_identity
+
+BF16 = mybir.dt.bfloat16
+F32 = mybir.dt.float32
+U32 = mybir.dt.uint32
+U8 = mybir.dt.uint8
+FP8X4 = mybir.dt.float8_e4m3fn_x4
+ALU = mybir.AluOpType
+FUNC = mybir.ActivationFunctionType
+AXIS = mybir.AxisListType
+
+P = 128
+SEQ = 1024
+HEADS = 4
+DIM = 128
+ROW = HEADS * DIM
+PAIR_DIM = 2 * DIM
+PACK = 4
+K_PASS = P * PACK
+TILES_PER_PASS = K_PASS // P
+PASSES = SEQ // K_PASS
+Q_TILES = SEQ // P
+UNITS = Q_TILES * HEADS
+PAIR_UNITS = UNITS // 2
+
+SCALE = 1.0 / math.sqrt(DIM)
+LAMBDA_INIT = 0.8 - 0.6 * math.exp(-0.3 * 12)
+NEG_INF = -1e30
+EPS = 1e-5
+
+FLOPS = 2 * HEADS * (512 * 512 + 512 * 1024) * (DIM + PAIR_DIM)
+
+
+def passes_of(q_tile):
+    return q_tile // TILES_PER_PASS + 1
+
+
+def tile_refphi4flashdiffattention_pa_kernel(
+    tc, q, k, v, lambda_q1, lambda_k1, lambda_q2, lambda_k2, subln_weight, out
+):
+    nc = tc.nc
+
+    q_rows = q.rearrange("b (j p) h d -> p (b j) (h d)", p=P)
+    k_rows = k.rearrange("b (j p) h d -> p (b j) (h d)", p=P)
+    out_rows = out.rearrange("b (j p) h d -> p (b j) (h d)", p=P)
+    v_rows = v.rearrange("b (m p e) h d -> p (b m) (e h d)", p=P, e=2)
+
+    with ExitStack() as stack:
+        keep = stack.enter_context(tc.tile_pool(name="keep", bufs=1))
+        work = stack.enter_context(tc.tile_pool(name="work", bufs=4))
+        small = stack.enter_context(tc.tile_pool(name="small", bufs=6))
+        ps_s = stack.enter_context(tc.psum_pool(name="ps_s", bufs=4))
+        ps_t = stack.enter_context(tc.psum_pool(name="ps_t", bufs=2))
+        ps_o = stack.enter_context(tc.psum_pool(name="ps_o", bufs=2))
+
+        q_sb = [keep.tile([P, ROW], BF16, name="q_sb%d" % j) for j in range(Q_TILES)]
+        k_sb = [keep.tile([P, ROW], BF16, name="k_sb%d" % j) for j in range(Q_TILES)]
+        v_raw = [keep.tile([P, PACK, ROW], BF16, name="v_raw%d" % g) for g in range(PASSES)]
+
+        def load_rows(j):
+            nc.sync.dma_start(out=k_sb[j][:], in_=k_rows[:, j, :])
+            nc.sync.dma_start(out=q_sb[j][:], in_=q_rows[:, j, :])
+
+        def load_values(g):
+            nc.sync.dma_start(
+                out=v_raw[g][:].rearrange("p (u e) c -> p u (e c)", e=2),
+                in_=v_rows[:, 2 * g : 2 * g + 2, :],
+            )
+
+        for j in range(Q_TILES):
+            load_rows(j)
+            if j % TILES_PER_PASS == 0:
+                load_values(j // TILES_PER_PASS)
+
+        lam_in = keep.tile([P, 4, DIM], BF16, name="lam_in")
+        for slot, vector in enumerate((lambda_q1, lambda_q2, lambda_k1, lambda_k2)):
+            nc.scalar.dma_start(out=lam_in[:, slot, :], in_=vector.partition_broadcast(P))
+        weight_bf = keep.tile([P, PAIR_DIM], BF16, name="weight_bf")
+        nc.scalar.dma_start(out=weight_bf[:], in_=subln_weight.partition_broadcast(P))
+
+        ident_bf = keep.tile([P, P], BF16, name="ident_bf")
+        make_identity(nc, ident_bf[:])
+        mask_f32 = keep.tile([P, P], F32, name="mask_f32")
+        nc.gpsimd.memset(mask_f32[:], 0.0)
+        nc.gpsimd.affine_select(
+            out=mask_f32[:],
+            in_=mask_f32[:],
+            pattern=[[-1, P]],
+            compare_op=ALU.is_ge,
+            fill=NEG_INF,
+            base=0,
+            channel_multiplier=1,
+        )
+        mask_bf = keep.tile([P, P], BF16, name="mask_bf")
+        nc.vector.tensor_copy(out=mask_bf[:], in_=mask_f32[:])
+        ident_f32 = keep.tile([P, P], F32, name="ident_f32")
+        make_identity(nc, ident_f32[:])
+        minus_one = keep.tile([P, 2], F32, name="minus_one")
+        nc.gpsimd.memset(minus_one[:], -1.0)
+        minus_half = keep.tile([P, 1], F32, name="minus_half")
+        nc.gpsimd.memset(minus_half[:], -0.5)
+
+        e_tiles = []
+        for i in range(Q_TILES):
+            width = passes_of(i) * K_PASS
+            e_tile = keep.tile([P, HEADS, width], BF16, name="e_tile%d" % i)
+            seen = (i + 1) * P
+            if seen < width:
+                nc.vector.memset(e_tile[:, :, seen:width], 0.0)
+            e_tiles.append(e_tile)
+
+        products = keep.tile([P, 2, DIM], F32, name="products")
+        nc.gpsimd.tensor_tensor(
+            out=products[:], in0=lam_in[:, 0:2, :], in1=lam_in[:, 2:4, :], op=ALU.mult
+        )
+        unread = keep.tile([P, 2, DIM], F32, name="unread")
+        dots = keep.tile([P, 2], F32, name="dots")
+        for term in range(2):
+            nc.scalar.activation(
+                out=unread[:, term, :],
+                in_=products[:, term, :],
+                func=FUNC.Copy,
+                accum_out=dots[:, term : term + 1],
+            )
+        powers = keep.tile([P, 2], F32, name="powers")
+        nc.scalar.activation(out=powers[:], in_=dots[:], func=FUNC.Exp)
+        difference = keep.tile([P, 1], F32, name="difference")
+        nc.gpsimd.tensor_tensor(
+            out=difference[:], in0=powers[:, 1:2], in1=powers[:, 0:1], op=ALU.subtract
+        )
+        signs = keep.tile([P, 2], F32, name="signs")
+        nc.gpsimd.memset(signs[:, 0:1], 1.0)
+        nc.gpsimd.tensor_scalar_add(out=signs[:, 1:2], in0=difference[:], scalar1=-LAMBDA_INIT)
+
+        gain = keep.tile([P, PAIR_DIM], F32, name="gain")
+        nc.gpsimd.tensor_scalar(
+            out=gain[:],
+            in0=weight_bf[:],
+            scalar1=(1.0 - LAMBDA_INIT) * math.sqrt(PAIR_DIM),
+            scalar2=0.0,
+            op0=ALU.mult,
+            op1=ALU.add,
+        )
+
+        v_grouped = [
+            keep.tile([P, ROW * PACK], BF16, name="v_grouped%d" % g, align_bytes=64)
+            for g in range(PASSES)
+        ]
+        v_codes = [
+            keep.tile([P, ROW], U32, name="v_codes%d" % g, align_bytes=64) for g in range(PASSES)
+        ]
+        v_scales = [
+            keep.tile([P, ROW], U8, name="v_scales%d" % g, align_bytes=64) for g in range(PASSES)
+        ]
+
+        def regroup_values(g):
+            nc.vector.tensor_copy(
+                out=v_grouped[g][:].rearrange("p (c i t) -> p c t i", i=4, t=PACK),
+                in_=v_raw[g][:].rearrange("p t (c i) -> p c t i", i=4),
+            )
+
+        def quantise_values(g):
+            nc.vector.quantize_mx(
+                out=v_codes[g][:].bitcast(FP8X4), scales=v_scales[g][:], in_=v_grouped[g][:]
+            )
+
+        q_turned = [keep.tile([P, HEADS, P], BF16, name="q_turned%d" % j) for j in range(Q_TILES)]
+        k_turned = [keep.tile([P, HEADS, K_PASS], BF16, name="k_turned%d" % g) for g in range(PASSES)]
+        rows_ps = {}
+
+        def turn_rows(j):
+            bank = ps_t.tile([P, 2, HEADS, P], BF16, name="rows_bank", tag="t")
+            for h in range(HEADS):
+                cols = slice(h * DIM, (h + 1) * DIM)
+                nc.tensor.transpose(bank[:, 0, h, :], q_sb[j][:, cols], ident_bf[:])
+                nc.tensor.transpose(bank[:, 1, h, :], k_sb[j][:, cols], ident_bf[:])
+            rows_ps[j] = bank
+
+        def copy_rows(j):
+            g, t = divmod(j, TILES_PER_PASS)
+            nc.vector.tensor_copy(out=q_turned[j][:], in_=rows_ps[j][:, 0, :, :])
+            nc.vector.tensor_copy(
+                out=k_turned[g][:, :, t * P : (t + 1) * P], in_=rows_ps[j][:, 1, :, :]
+            )
+
+        s_banks = {}
+        tops = {}
+        shifts = {}
+        row_sums = {}
+        e_banks = {}
+        e_grouped = {}
+        e_codes = {}
+        e_scales = {}
+        o_banks = {}
+
+        def scores(n):
+            i, h = divmod(n, HEADS)
+            banks = []
+            for g in range(passes_of(i)):
+                width = min(i + 1 - g * TILES_PER_PASS, TILES_PER_PASS) * P
+                holds_diagonal = g == passes_of(i) - 1
+                bank = ps_s.tile([P, K_PASS], F32, name="s_bank")
+                nc.tensor.matmul(
+                    out=bank[:, 0:width],
+                    lhsT=q_turned[i][:, h, :],
+                    rhs=k_turned[g][:, h, 0:width],
+                    start=True,
+                    stop=not holds_diagonal,
+                )
+                if holds_diagonal:
+                    nc.tensor.matmul(
+                        out=bank[:, width - P : width],
+                        lhsT=ident_bf[:],
+                        rhs=mask_bf[:],
+                        start=False,
+                        stop=True,
+                    )
+                banks.append((bank, width))
+            s_banks[n] = banks
+
+        def row_tops(n):
+            top = small.tile([P, PASSES], F32, name="top")
+            for g, (bank, width) in enumerate(s_banks[n]):
+                nc.vector.tensor_reduce(
+                    out=top[:, g : g + 1], in_=bank[:, 0:width], axis=AXIS.X, op=ALU.max
+                )
+            tops[n] = top
+
+        def shift(n):
+            bias = small.tile([P, 1], F32, name="bias")
+            if len(s_banks[n]) == 2:
+                nc.vector.tensor_scalar(
+                    out=bias[:],
+                    in0=tops[n][:, 0:1],
+                    scalar1=tops[n][:, 1:2],
+                    scalar2=-SCALE,
+                    op0=ALU.max,
+                    op1=ALU.mult,
+                )
+            else:
+                nc.vector.tensor_scalar_mul(out=bias[:], in0=tops[n][:, 0:1], scalar1=-SCALE)
+            shifts[n] = bias
+
+        def exponent(n):
+            i, h = divmod(n, HEADS)
+            m, half = divmod(n, 2)
+            if half == 0:
+                row_sums[m] = small.tile([P, 2, passes_of(i)], F32, name="row_sum")
+            for g, (bank, width) in enumerate(s_banks[n]):
+                nc.scalar.activation(
+                    out=e_tiles[i][:, h, g * K_PASS : g * K_PASS + width],
+                    in_=bank[:, 0:width],
+                    func=FUNC.Exp,
+                    bias=shifts[n][:, 0:1],
+                    scale=SCALE,
+                    accum_out=row_sums[m][:, half, g : g + 1],
+                )
+
+        def turn(n):
+            i, h = divmod(n, HEADS)
+            words = e_tiles[i][:, h, :].bitcast(F32)
+            bank = ps_t.tile([P, passes_of(i), 2, P], F32, name="e_bank", tag="t")
+            for g in range(passes_of(i)):
+                for u in range(2):
+                    first = (2 * g + u) * P
+                    nc.tensor.transpose(bank[:, g, u, :], words[:, first : first + P], ident_f32[:])
+            e_banks[n] = bank
+
+        def regroup(n):
+            passes = passes_of(n // HEADS)
+            grouped = work.tile([P, passes * K_PASS], BF16, name="grouped", align_bytes=64)
+            nc.scalar.copy(
+                out=grouped[:].bitcast(F32).rearrange("p (g r u) -> p g r u", g=passes, u=2),
+                in_=e_banks[n][:].rearrange("p g u r -> p g r u"),
+            )
+            e_grouped[n] = grouped
+
+        def quantise(n):
+            passes = passes_of(n // HEADS)
+            codes = work.tile([P, passes * P], U32, name="codes", align_bytes=64)
+            scales = work.tile([P, passes * P], U8, name="scales", align_bytes=64)
+            nc.vector.quantize_mx(out=codes[:].bitcast(FP8X4), scales=scales[:], in_=e_grouped[n][:])
+            e_codes[n] = codes
+            e_scales[n] = scales
+
+        def attend(n):
+            i, h = divmod(n, HEADS)
+            m, half = divmod(n, 2)
+            if half == 0:
+                o_banks[m] = ps_o.tile([P, 2, PAIR_DIM], F32, name="o_bank")
+            features = slice((h // 2) * PAIR_DIM, (h // 2 + 1) * PAIR_DIM)
+            for g in range(passes_of(i)):
+                queries = slice(g * P, (g + 1) * P)
+                nc.tensor.matmul_mx(
+                    out=o_banks[m][:, half, :],
+                    lhsT=e_codes[n][:, queries].bitcast(FP8X4),
+                    lhsT_scale=e_scales[n][:, queries],
+                    rhs=v_codes[g][:, features].bitcast(FP8X4),
+                    rhs_scale=v_scales[g][:, features],
+                    start=(g == 0),
+                    stop=(g == passes_of(i) - 1),
+                )
+
+        factors = {}
+        seconds = {}
+        xs = {}
+        rstds = {}
+
+        def weigh(m):
+            sums = row_sums[m]
+            total = sums[:, :, 0]
+            if passes_of(m // 2) == 2:
+                added = small.tile([P, 2], F32, name="added")
+                nc.gpsimd.tensor_tensor(out=added[:], in0=sums[:, :, 0], in1=sums[:, :, 1], op=ALU.add)
+                total = added[:]
+            inverse = small.tile([P, 2], F32, name="inverse")
+            nc.gpsimd.tensor_tensor(out=inverse[:], in0=total, in1=minus_one[:], op=ALU.pow)
+            factor = small.tile([P, 2], F32, name="factor")
+            nc.gpsimd.tensor_tensor(out=factor[:], in0=inverse[:], in1=signs[:], op=ALU.mult)
+            factors[m] = factor
+
+        def scale_second(m):
+            second = work.tile([P, PAIR_DIM], F32, name="second")
+            nc.scalar.activation(
+                out=second[:], in_=o_banks[m][:, 1, :], func=FUNC.Copy, scale=factors[m][:, 1:2]
+            )
+            seconds[m] = second
+
+        def combine(m):
+            x = work.tile([P, PAIR_DIM], F32, name="x")
+            nc.vector.scalar_tensor_tensor(
+                out=x[:],
+                in0=o_banks[m][:, 0, :],
+                scalar=factors[m][:, 0:1],
+                in1=seconds[m][:],
+                op0=ALU.mult,
+                op1=ALU.add,
+            )
+            xs[m] = x
+
+        def measure(m):
+            squares = work.tile([P, PAIR_DIM], F32, name="squares")
+            sum_sq = small.tile([P, 1], F32, name="sum_sq")
+            nc.scalar.activation(out=squares[:], in_=xs[m][:], func=FUNC.Square, accum_out=sum_sq[:])
+            floored = small.tile([P, 1], F32, name="floored")
+            nc.gpsimd.tensor_scalar_add(out=floored[:], in0=sum_sq[:], scalar1=PAIR_DIM * EPS)
+            rstd = small.tile([P, 1], F32, name="rstd")
+            nc.gpsimd.tensor_tensor(out=rstd[:], in0=floored[:], in1=minus_half[:], op=ALU.pow)
+            rstds[m] = rstd
+
+        def finish(m):
+            i, pair = divmod(m, 2)
+            y = work.tile([P, PAIR_DIM], F32, name="y")
+            nc.vector.scalar_tensor_tensor(
+                out=y[:],
+                in0=xs[m][:],
+                scalar=rstds[m][:, 0:1],
+                in1=gain[:],
+                op0=ALU.mult,
+                op1=ALU.mult,
+            )
+            nc.sync.dma_start(
+                out=out_rows[:, i, pair * PAIR_DIM : (pair + 1) * PAIR_DIM], in_=y[:]
+            )
+
+        def run(stage, index, count):
+            if 0 <= index < count:
+                stage(index)
+
+        def run_pair(stage, n, lag):
+            if (n - lag) % 2 == 0:
+                run(stage, (n - lag) // 2, PAIR_UNITS)
+
+        def tick(n):
+            run_pair(scale_second, n, 5)
+            run_pair(measure, n, 7)
+            run(exponent, n, UNITS)
+            run(regroup, n - 1, UNITS)
+            run(row_tops, n + 1, UNITS)
+            run(quantise, n - 2, UNITS)
+            run(shift, n + 1, UNITS)
+            run_pair(combine, n, 5)
+            run_pair(finish, n, 9)
+            if n % HEADS == 1:
+                run(copy_rows, n // HEADS + 1, Q_TILES)
+            round_of_pass = HEADS * TILES_PER_PASS
+            if (n + 1) % round_of_pass == 0:
+                run(regroup_values, (n + 1) // round_of_pass, PASSES)
+            if n % round_of_pass == 0:
+                run(quantise_values, n // round_of_pass, PASSES)
+            run_pair(weigh, n, 2)
+            run(scores, n + 2, UNITS)
+            run(turn, n, UNITS)
+            run(attend, n - 2, UNITS)
+            if n % HEADS == 0:
+                run(turn_rows, n // HEADS + 1, Q_TILES)
+
+        first_tick = -HEADS
+        last_tick = 2 * (PAIR_UNITS - 1) + 9
+        with tc.manual_schedule():
+            for n in range(first_tick, last_tick + 1):
+                tick(n)

@@ -73,14 +73,32 @@ def tile_refphi4flashdiffattention_pa_kernel(
 
         for j in range(Q_TILES):
             load_rows(j)
-            if j % TILES_PER_PASS == 0:
+            if j % TILES_PER_PASS == 1:
                 load_values(j // TILES_PER_PASS)
 
-        lam_in = keep.tile([P, 4, DIM], BF16, name="lam_in")
+        first_row = keep.tile([P, 4 * DIM + PAIR_DIM], BF16, name="first_row")
+        nc.vector.memset(first_row[:], 0.0)
         for slot, vector in enumerate((lambda_q1, lambda_q2, lambda_k1, lambda_k2)):
-            nc.scalar.dma_start(out=lam_in[:, slot, :], in_=vector.partition_broadcast(P))
-        weight_bf = keep.tile([P, PAIR_DIM], BF16, name="weight_bf")
-        nc.scalar.dma_start(out=weight_bf[:], in_=subln_weight.partition_broadcast(P))
+            nc.scalar.dma_start(
+                out=first_row[0:1, slot * DIM : (slot + 1) * DIM], in_=vector.unsqueeze(0)
+            )
+        nc.scalar.dma_start(out=first_row[0:1, 4 * DIM :], in_=subln_weight.unsqueeze(0))
+        ones = keep.tile([P, P], BF16, name="ones")
+        nc.vector.memset(ones[:], 1.0)
+        lam_bank = ps_s.tile([P, 4, DIM], F32, name="lam_bank", tag="s_bank")
+        nc.tensor.matmul(
+            out=lam_bank[:].rearrange("p s d -> p (s d)"),
+            lhsT=ones[:],
+            rhs=first_row[:, 0 : 4 * DIM],
+            start=True,
+            stop=True,
+        )
+        weight_bank = ps_s.tile([P, PAIR_DIM], F32, name="weight_bank", tag="s_bank")
+        nc.tensor.matmul(
+            out=weight_bank[:], lhsT=ones[:], rhs=first_row[:, 4 * DIM :], start=True, stop=True
+        )
+        lam_in = keep.tile([P, 4, DIM], F32, name="lam_in")
+        nc.scalar.copy(out=lam_in[:], in_=lam_bank[:])
 
         ident_bf = keep.tile([P, P], BF16, name="ident_bf")
         make_identity(nc, ident_bf[:])
@@ -137,14 +155,7 @@ def tile_refphi4flashdiffattention_pa_kernel(
         nc.gpsimd.tensor_scalar_add(out=signs[:, 1:2], in0=difference[:], scalar1=-LAMBDA_INIT)
 
         gain = keep.tile([P, PAIR_DIM], F32, name="gain")
-        nc.gpsimd.tensor_scalar(
-            out=gain[:],
-            in0=weight_bf[:],
-            scalar1=(1.0 - LAMBDA_INIT) * math.sqrt(PAIR_DIM),
-            scalar2=0.0,
-            op0=ALU.mult,
-            op1=ALU.add,
-        )
+        nc.scalar.mul(out=gain[:], in_=weight_bank[:], mul=(1.0 - LAMBDA_INIT) * math.sqrt(PAIR_DIM))
 
         v_grouped = [
             keep.tile([P, ROW * PACK], BF16, name="v_grouped%d" % g, align_bytes=64)
@@ -384,9 +395,9 @@ def tile_refphi4flashdiffattention_pa_kernel(
             run(quantise, n - 2, UNITS)
             run(shift, n + 1, UNITS)
             run_pair(combine, n, 5)
-            run_pair(finish, n, 9)
+            run_pair(finish, n, 11)
             if n % HEADS == 1:
-                run(copy_rows, n // HEADS + 1, Q_TILES)
+                run(copy_rows, n // HEADS + 2, Q_TILES)
             round_of_pass = HEADS * TILES_PER_PASS
             if (n + 1) % round_of_pass == 0:
                 run(regroup_values, (n + 1) // round_of_pass, PASSES)
@@ -397,10 +408,10 @@ def tile_refphi4flashdiffattention_pa_kernel(
             run(turn, n, UNITS)
             run(attend, n - 2, UNITS)
             if n % HEADS == 0:
-                run(turn_rows, n // HEADS + 1, Q_TILES)
+                run(turn_rows, n // HEADS + 2, Q_TILES)
 
-        first_tick = -HEADS
-        last_tick = 2 * (PAIR_UNITS - 1) + 9
+        first_tick = -2 * HEADS
+        last_tick = 2 * (PAIR_UNITS - 1) + 11
         with tc.manual_schedule():
             for n in range(first_tick, last_tick + 1):
                 tick(n)

@@ -32,6 +32,8 @@ LAMBDA_INIT = 0.8 - 0.6 * math.exp(-0.3 * 12)
 NEG_INF = -1e30
 EPS = 1e-5
 
+LAM_TICK = -3
+
 FLOPS = 2 * HEADS * (512 * 512 + 512 * 1024) * (DIM + PAIR_DIM)
 
 
@@ -57,6 +59,14 @@ def tile_refphi4flashdiffattention_pa_kernel(
         ps_t = stack.enter_context(tc.psum_pool(name="ps_t", bufs=2))
         ps_o = stack.enter_context(tc.psum_pool(name="ps_o", bufs=2))
 
+        first_row = keep.tile([P, 4 * DIM + PAIR_DIM], BF16, name="first_row")
+        nc.vector.memset(first_row[:], 0.0)
+        for slot, vector in enumerate((lambda_q1, lambda_q2, lambda_k1, lambda_k2)):
+            nc.scalar.dma_start(
+                out=first_row[0:1, slot * DIM : (slot + 1) * DIM], in_=vector.unsqueeze(0)
+            )
+        nc.scalar.dma_start(out=first_row[0:1, 4 * DIM :], in_=subln_weight.unsqueeze(0))
+
         q_sb = [keep.tile([P, ROW], BF16, name="q_sb%d" % j) for j in range(Q_TILES)]
         k_sb = [keep.tile([P, ROW], BF16, name="k_sb%d" % j) for j in range(Q_TILES)]
         v_raw = [keep.tile([P, PACK, ROW], BF16, name="v_raw%d" % g) for g in range(PASSES)]
@@ -75,30 +85,6 @@ def tile_refphi4flashdiffattention_pa_kernel(
             load_rows(j)
             if j % TILES_PER_PASS == 1:
                 load_values(j // TILES_PER_PASS)
-
-        first_row = keep.tile([P, 4 * DIM + PAIR_DIM], BF16, name="first_row")
-        nc.vector.memset(first_row[:], 0.0)
-        for slot, vector in enumerate((lambda_q1, lambda_q2, lambda_k1, lambda_k2)):
-            nc.scalar.dma_start(
-                out=first_row[0:1, slot * DIM : (slot + 1) * DIM], in_=vector.unsqueeze(0)
-            )
-        nc.scalar.dma_start(out=first_row[0:1, 4 * DIM :], in_=subln_weight.unsqueeze(0))
-        ones = keep.tile([P, P], BF16, name="ones")
-        nc.vector.memset(ones[:], 1.0)
-        lam_bank = ps_s.tile([P, 4, DIM], F32, name="lam_bank", tag="s_bank")
-        nc.tensor.matmul(
-            out=lam_bank[:].rearrange("p s d -> p (s d)"),
-            lhsT=ones[:],
-            rhs=first_row[:, 0 : 4 * DIM],
-            start=True,
-            stop=True,
-        )
-        weight_bank = ps_s.tile([P, PAIR_DIM], F32, name="weight_bank", tag="s_bank")
-        nc.tensor.matmul(
-            out=weight_bank[:], lhsT=ones[:], rhs=first_row[:, 4 * DIM :], start=True, stop=True
-        )
-        lam_in = keep.tile([P, 4, DIM], F32, name="lam_in")
-        nc.scalar.copy(out=lam_in[:], in_=lam_bank[:])
 
         ident_bf = keep.tile([P, P], BF16, name="ident_bf")
         make_identity(nc, ident_bf[:])
@@ -131,31 +117,63 @@ def tile_refphi4flashdiffattention_pa_kernel(
                 nc.vector.memset(e_tile[:, :, seen:width], 0.0)
             e_tiles.append(e_tile)
 
+        ones = keep.tile([P, P], BF16, name="ones")
+        nc.vector.memset(ones[:], 1.0)
+        lam_in = keep.tile([P, 4, DIM], F32, name="lam_in")
         products = keep.tile([P, 2, DIM], F32, name="products")
-        nc.gpsimd.tensor_tensor(
-            out=products[:], in0=lam_in[:, 0:2, :], in1=lam_in[:, 2:4, :], op=ALU.mult
-        )
         unread = keep.tile([P, 2, DIM], F32, name="unread")
         dots = keep.tile([P, 2], F32, name="dots")
-        for term in range(2):
-            nc.scalar.activation(
-                out=unread[:, term, :],
-                in_=products[:, term, :],
-                func=FUNC.Copy,
-                accum_out=dots[:, term : term + 1],
-            )
         powers = keep.tile([P, 2], F32, name="powers")
-        nc.scalar.activation(out=powers[:], in_=dots[:], func=FUNC.Exp)
         difference = keep.tile([P, 1], F32, name="difference")
-        nc.gpsimd.tensor_tensor(
-            out=difference[:], in0=powers[:, 1:2], in1=powers[:, 0:1], op=ALU.subtract
-        )
         signs = keep.tile([P, 2], F32, name="signs")
         nc.gpsimd.memset(signs[:, 0:1], 1.0)
-        nc.gpsimd.tensor_scalar_add(out=signs[:, 1:2], in0=difference[:], scalar1=-LAMBDA_INIT)
-
         gain = keep.tile([P, PAIR_DIM], F32, name="gain")
-        nc.scalar.mul(out=gain[:], in_=weight_bank[:], mul=(1.0 - LAMBDA_INIT) * math.sqrt(PAIR_DIM))
+        spread_banks = {}
+
+        def spread_vectors():
+            lam_bank = ps_s.tile([P, 4, DIM], F32, name="lam_bank", tag="s_bank")
+            nc.tensor.matmul(
+                out=lam_bank[:].rearrange("p s d -> p (s d)"),
+                lhsT=ones[:],
+                rhs=first_row[:, 0 : 4 * DIM],
+                start=True,
+                stop=True,
+            )
+            weight_bank = ps_s.tile([P, PAIR_DIM], F32, name="weight_bank", tag="s_bank")
+            nc.tensor.matmul(
+                out=weight_bank[:], lhsT=ones[:], rhs=first_row[:, 4 * DIM :], start=True, stop=True
+            )
+            spread_banks["lam"] = lam_bank
+            spread_banks["weight"] = weight_bank
+
+        def lam_products():
+            nc.scalar.copy(out=lam_in[:], in_=spread_banks["lam"][:])
+            nc.gpsimd.tensor_tensor(
+                out=products[:], in0=lam_in[:, 0:2, :], in1=lam_in[:, 2:4, :], op=ALU.mult
+            )
+
+        def scale_gain():
+            nc.scalar.mul(
+                out=gain[:],
+                in_=spread_banks["weight"][:],
+                mul=(1.0 - LAMBDA_INIT) * math.sqrt(PAIR_DIM),
+            )
+
+        def lam_dots():
+            for term in range(2):
+                nc.scalar.activation(
+                    out=unread[:, term, :],
+                    in_=products[:, term, :],
+                    func=FUNC.Copy,
+                    accum_out=dots[:, term : term + 1],
+                )
+
+        def lam_signs():
+            nc.scalar.activation(out=powers[:], in_=dots[:], func=FUNC.Exp)
+            nc.gpsimd.tensor_tensor(
+                out=difference[:], in0=powers[:, 1:2], in1=powers[:, 0:1], op=ALU.subtract
+            )
+            nc.gpsimd.tensor_scalar_add(out=signs[:, 1:2], in0=difference[:], scalar1=-LAMBDA_INIT)
 
         v_grouped = [
             keep.tile([P, ROW * PACK], BF16, name="v_grouped%d" % g, align_bytes=64)
@@ -391,6 +409,14 @@ def tile_refphi4flashdiffattention_pa_kernel(
             run_pair(measure, n, 7)
             run(exponent, n, UNITS)
             run(regroup, n - 1, UNITS)
+            if n == LAM_TICK + 1:
+                lam_products()
+            if n == LAM_TICK + 2:
+                scale_gain()
+            if n == LAM_TICK + 3:
+                lam_dots()
+            if n == LAM_TICK + 4:
+                lam_signs()
             run(row_tops, n + 1, UNITS)
             run(quantise, n - 2, UNITS)
             run(shift, n + 1, UNITS)
@@ -409,6 +435,8 @@ def tile_refphi4flashdiffattention_pa_kernel(
             run(attend, n - 2, UNITS)
             if n % HEADS == 0:
                 run(turn_rows, n // HEADS + 2, Q_TILES)
+            if n == LAM_TICK:
+                spread_vectors()
 
         first_tick = -2 * HEADS
         last_tick = 2 * (PAIR_UNITS - 1) + 11

import math
from contextlib import ExitStack

import concourse.mybir as mybir
from concourse.masks import make_identity

BF16 = mybir.dt.bfloat16
F32 = mybir.dt.float32
U32 = mybir.dt.uint32
U8 = mybir.dt.uint8
FP8X4 = mybir.dt.float8_e4m3fn_x4
ALU = mybir.AluOpType
FUNC = mybir.ActivationFunctionType
AXIS = mybir.AxisListType

P = 128
SEQ = 1024
HEADS = 4
DIM = 128
ROW = HEADS * DIM
PAIR_DIM = 2 * DIM
PACK = 4
K_PASS = P * PACK
TILES_PER_PASS = K_PASS // P
PASSES = SEQ // K_PASS
Q_TILES = SEQ // P
UNITS = Q_TILES * HEADS
PAIR_UNITS = UNITS // 2

SCALE = 1.0 / math.sqrt(DIM)
LAMBDA_INIT = 0.8 - 0.6 * math.exp(-0.3 * 12)
NEG_INF = -1e30
EPS = 1e-5

LAM_TICK = -3

FLOPS = 2 * HEADS * (512 * 512 + 512 * 1024) * (DIM + PAIR_DIM)


def passes_of(q_tile):
    return q_tile // TILES_PER_PASS + 1


def tile_refphi4flashdiffattention_pa_kernel(
    tc, q, k, v, lambda_q1, lambda_k1, lambda_q2, lambda_k2, subln_weight, out
):
    nc = tc.nc

    q_rows = q.rearrange("b (j p) h d -> p (b j) (h d)", p=P)
    k_rows = k.rearrange("b (j p) h d -> p (b j) (h d)", p=P)
    out_rows = out.rearrange("b (j p) h d -> p (b j) (h d)", p=P)
    v_rows = v.rearrange("b (m p e) h d -> p (b m) (e h d)", p=P, e=2)

    with ExitStack() as stack:
        keep = stack.enter_context(tc.tile_pool(name="keep", bufs=1))
        work = stack.enter_context(tc.tile_pool(name="work", bufs=4))
        small = stack.enter_context(tc.tile_pool(name="small", bufs=6))
        ps_s = stack.enter_context(tc.psum_pool(name="ps_s", bufs=4))
        ps_t = stack.enter_context(tc.psum_pool(name="ps_t", bufs=2))
        ps_o = stack.enter_context(tc.psum_pool(name="ps_o", bufs=2))

        first_row = keep.tile([P, 4 * DIM + PAIR_DIM], BF16, name="first_row")
        nc.vector.memset(first_row[:], 0.0)
        for slot, vector in enumerate((lambda_q1, lambda_q2, lambda_k1, lambda_k2)):
            nc.scalar.dma_start(
                out=first_row[0:1, slot * DIM : (slot + 1) * DIM], in_=vector.unsqueeze(0)
            )
        nc.scalar.dma_start(out=first_row[0:1, 4 * DIM :], in_=subln_weight.unsqueeze(0))

        q_sb = [keep.tile([P, ROW], BF16, name="q_sb%d" % j) for j in range(Q_TILES)]
        k_sb = [keep.tile([P, ROW], BF16, name="k_sb%d" % j) for j in range(Q_TILES)]
        v_raw = [keep.tile([P, PACK, ROW], BF16, name="v_raw%d" % g) for g in range(PASSES)]

        def load_rows(j):
            nc.sync.dma_start(out=k_sb[j][:], in_=k_rows[:, j, :])
            nc.sync.dma_start(out=q_sb[j][:], in_=q_rows[:, j, :])

        def load_values(g):
            nc.sync.dma_start(
                out=v_raw[g][:].rearrange("p (u e) c -> p u (e c)", e=2),
                in_=v_rows[:, 2 * g : 2 * g + 2, :],
            )

        for j in range(Q_TILES):
            load_rows(j)
            if j % TILES_PER_PASS == 1:
                load_values(j // TILES_PER_PASS)

        ident_bf = keep.tile([P, P], BF16, name="ident_bf")
        make_identity(nc, ident_bf[:])
        mask_f32 = keep.tile([P, P], F32, name="mask_f32")
        nc.gpsimd.memset(mask_f32[:], 0.0)
        nc.gpsimd.affine_select(
            out=mask_f32[:],
            in_=mask_f32[:],
            pattern=[[-1, P]],
            compare_op=ALU.is_ge,
            fill=NEG_INF,
            base=0,
            channel_multiplier=1,
        )
        mask_bf = keep.tile([P, P], BF16, name="mask_bf")
        nc.vector.tensor_copy(out=mask_bf[:], in_=mask_f32[:])
        ident_f32 = keep.tile([P, P], F32, name="ident_f32")
        make_identity(nc, ident_f32[:])
        minus_one = keep.tile([P, 2], F32, name="minus_one")
        nc.gpsimd.memset(minus_one[:], -1.0)
        minus_half = keep.tile([P, 1], F32, name="minus_half")
        nc.gpsimd.memset(minus_half[:], -0.5)

        e_tiles = []
        for i in range(Q_TILES):
            width = passes_of(i) * K_PASS
            e_tile = keep.tile([P, HEADS, width], BF16, name="e_tile%d" % i)
            seen = (i + 1) * P
            if seen < width:
                nc.vector.memset(e_tile[:, :, seen:width], 0.0)
            e_tiles.append(e_tile)

        ones = keep.tile([P, P], BF16, name="ones")
        nc.vector.memset(ones[:], 1.0)
        lam_in = keep.tile([P, 4, DIM], F32, name="lam_in")
        products = keep.tile([P, 2, DIM], F32, name="products")
        unread = keep.tile([P, 2, DIM], F32, name="unread")
        dots = keep.tile([P, 2], F32, name="dots")
        powers = keep.tile([P, 2], F32, name="powers")
        difference = keep.tile([P, 1], F32, name="difference")
        signs = keep.tile([P, 2], F32, name="signs")
        nc.gpsimd.memset(signs[:, 0:1], 1.0)
        gain = keep.tile([P, PAIR_DIM], F32, name="gain")
        spread_banks = {}

        def spread_vectors():
            lam_bank = ps_s.tile([P, 4, DIM], F32, name="lam_bank", tag="s_bank")
            nc.tensor.matmul(
                out=lam_bank[:].rearrange("p s d -> p (s d)"),
                lhsT=ones[:],
                rhs=first_row[:, 0 : 4 * DIM],
                start=True,
                stop=True,
            )
            weight_bank = ps_s.tile([P, PAIR_DIM], F32, name="weight_bank", tag="s_bank")
            nc.tensor.matmul(
                out=weight_bank[:], lhsT=ones[:], rhs=first_row[:, 4 * DIM :], start=True, stop=True
            )
            spread_banks["lam"] = lam_bank
            spread_banks["weight"] = weight_bank

        def lam_products():
            nc.scalar.copy(out=lam_in[:], in_=spread_banks["lam"][:])
            nc.gpsimd.tensor_tensor(
                out=products[:], in0=lam_in[:, 0:2, :], in1=lam_in[:, 2:4, :], op=ALU.mult
            )

        def scale_gain():
            nc.scalar.mul(
                out=gain[:],
                in_=spread_banks["weight"][:],
                mul=(1.0 - LAMBDA_INIT) * math.sqrt(PAIR_DIM),
            )

        def lam_dots():
            for term in range(2):
                nc.scalar.activation(
                    out=unread[:, term, :],
                    in_=products[:, term, :],
                    func=FUNC.Copy,
                    accum_out=dots[:, term : term + 1],
                )

        def lam_signs():
            nc.scalar.activation(out=powers[:], in_=dots[:], func=FUNC.Exp)
            nc.gpsimd.tensor_tensor(
                out=difference[:], in0=powers[:, 1:2], in1=powers[:, 0:1], op=ALU.subtract
            )
            nc.gpsimd.tensor_scalar_add(out=signs[:, 1:2], in0=difference[:], scalar1=-LAMBDA_INIT)

        v_grouped = [
            keep.tile([P, ROW * PACK], BF16, name="v_grouped%d" % g, align_bytes=64)
            for g in range(PASSES)
        ]
        v_codes = [
            keep.tile([P, ROW], U32, name="v_codes%d" % g, align_bytes=64) for g in range(PASSES)
        ]
        v_scales = [
            keep.tile([P, ROW], U8, name="v_scales%d" % g, align_bytes=64) for g in range(PASSES)
        ]

        def regroup_values(g):
            nc.vector.tensor_copy(
                out=v_grouped[g][:].rearrange("p (c i t) -> p c t i", i=4, t=PACK),
                in_=v_raw[g][:].rearrange("p t (c i) -> p c t i", i=4),
            )

        def quantise_values(g):
            nc.vector.quantize_mx(
                out=v_codes[g][:].bitcast(FP8X4), scales=v_scales[g][:], in_=v_grouped[g][:]
            )

        q_turned = [keep.tile([P, HEADS, P], BF16, name="q_turned%d" % j) for j in range(Q_TILES)]
        k_turned = [keep.tile([P, HEADS, K_PASS], BF16, name="k_turned%d" % g) for g in range(PASSES)]
        rows_ps = {}

        def turn_rows(j):
            bank = ps_t.tile([P, 2, HEADS, P], BF16, name="rows_bank", tag="t")
            for h in range(HEADS):
                cols = slice(h * DIM, (h + 1) * DIM)
                nc.tensor.transpose(bank[:, 0, h, :], q_sb[j][:, cols], ident_bf[:])
                nc.tensor.transpose(bank[:, 1, h, :], k_sb[j][:, cols], ident_bf[:])
            rows_ps[j] = bank

        def copy_rows(j):
            g, t = divmod(j, TILES_PER_PASS)
            nc.vector.tensor_copy(out=q_turned[j][:], in_=rows_ps[j][:, 0, :, :])
            nc.vector.tensor_copy(
                out=k_turned[g][:, :, t * P : (t + 1) * P], in_=rows_ps[j][:, 1, :, :]
            )

        s_banks = {}
        tops = {}
        shifts = {}
        row_sums = {}
        e_banks = {}
        e_grouped = {}
        e_codes = {}
        e_scales = {}
        o_banks = {}

        def scores(n):
            i, h = divmod(n, HEADS)
            banks = []
            for g in range(passes_of(i)):
                width = min(i + 1 - g * TILES_PER_PASS, TILES_PER_PASS) * P
                holds_diagonal = g == passes_of(i) - 1
                bank = ps_s.tile([P, K_PASS], F32, name="s_bank")
                nc.tensor.matmul(
                    out=bank[:, 0:width],
                    lhsT=q_turned[i][:, h, :],
                    rhs=k_turned[g][:, h, 0:width],
                    start=True,
                    stop=not holds_diagonal,
                )
                if holds_diagonal:
                    nc.tensor.matmul(
                        out=bank[:, width - P : width],
                        lhsT=ident_bf[:],
                        rhs=mask_bf[:],
                        start=False,
                        stop=True,
                    )
                banks.append((bank, width))
            s_banks[n] = banks

        def row_tops(n):
            top = small.tile([P, PASSES], F32, name="top")
            for g, (bank, width) in enumerate(s_banks[n]):
                nc.vector.tensor_reduce(
                    out=top[:, g : g + 1], in_=bank[:, 0:width], axis=AXIS.X, op=ALU.max
                )
            tops[n] = top

        def shift(n):
            bias = small.tile([P, 1], F32, name="bias")
            if len(s_banks[n]) == 2:
                nc.vector.tensor_scalar(
                    out=bias[:],
                    in0=tops[n][:, 0:1],
                    scalar1=tops[n][:, 1:2],
                    scalar2=-SCALE,
                    op0=ALU.max,
                    op1=ALU.mult,
                )
            else:
                nc.vector.tensor_scalar_mul(out=bias[:], in0=tops[n][:, 0:1], scalar1=-SCALE)
            shifts[n] = bias

        def exponent(n):
            i, h = divmod(n, HEADS)
            m, half = divmod(n, 2)
            if half == 0:
                row_sums[m] = small.tile([P, 2, passes_of(i)], F32, name="row_sum")
            for g, (bank, width) in enumerate(s_banks[n]):
                nc.scalar.activation(
                    out=e_tiles[i][:, h, g * K_PASS : g * K_PASS + width],
                    in_=bank[:, 0:width],
                    func=FUNC.Exp,
                    bias=shifts[n][:, 0:1],
                    scale=SCALE,
                    accum_out=row_sums[m][:, half, g : g + 1],
                )

        def turn(n):
            i, h = divmod(n, HEADS)
            words = e_tiles[i][:, h, :].bitcast(F32)
            bank = ps_t.tile([P, passes_of(i), 2, P], F32, name="e_bank", tag="t")
            for g in range(passes_of(i)):
                for u in range(2):
                    first = (2 * g + u) * P
                    nc.tensor.transpose(bank[:, g, u, :], words[:, first : first + P], ident_f32[:])
            e_banks[n] = bank

        def regroup(n):
            passes = passes_of(n // HEADS)
            grouped = work.tile([P, passes * K_PASS], BF16, name="grouped", align_bytes=64)
            nc.scalar.copy(
                out=grouped[:].bitcast(F32).rearrange("p (g r u) -> p g r u", g=passes, u=2),
                in_=e_banks[n][:].rearrange("p g u r -> p g r u"),
            )
            e_grouped[n] = grouped

        def quantise(n):
            passes = passes_of(n // HEADS)
            codes = work.tile([P, passes * P], U32, name="codes", align_bytes=64)
            scales = work.tile([P, passes * P], U8, name="scales", align_bytes=64)
            nc.vector.quantize_mx(out=codes[:].bitcast(FP8X4), scales=scales[:], in_=e_grouped[n][:])
            e_codes[n] = codes
            e_scales[n] = scales

        def attend(n):
            i, h = divmod(n, HEADS)
            m, half = divmod(n, 2)
            if half == 0:
                o_banks[m] = ps_o.tile([P, 2, PAIR_DIM], F32, name="o_bank")
            features = slice((h // 2) * PAIR_DIM, (h // 2 + 1) * PAIR_DIM)
            for g in range(passes_of(i)):
                queries = slice(g * P, (g + 1) * P)
                nc.tensor.matmul_mx(
                    out=o_banks[m][:, half, :],
                    lhsT=e_codes[n][:, queries].bitcast(FP8X4),
                    lhsT_scale=e_scales[n][:, queries],
                    rhs=v_codes[g][:, features].bitcast(FP8X4),
                    rhs_scale=v_scales[g][:, features],
                    start=(g == 0),
                    stop=(g == passes_of(i) - 1),
                )

        factors = {}
        seconds = {}
        xs = {}
        rstds = {}

        def weigh(m):
            sums = row_sums[m]
            total = sums[:, :, 0]
            if passes_of(m // 2) == 2:
                added = small.tile([P, 2], F32, name="added")
                nc.gpsimd.tensor_tensor(out=added[:], in0=sums[:, :, 0], in1=sums[:, :, 1], op=ALU.add)
                total = added[:]
            inverse = small.tile([P, 2], F32, name="inverse")
            nc.gpsimd.tensor_tensor(out=inverse[:], in0=total, in1=minus_one[:], op=ALU.pow)
            factor = small.tile([P, 2], F32, name="factor")
            nc.gpsimd.tensor_tensor(out=factor[:], in0=inverse[:], in1=signs[:], op=ALU.mult)
            factors[m] = factor

        def scale_second(m):
            second = work.tile([P, PAIR_DIM], F32, name="second")
            nc.scalar.activation(
                out=second[:], in_=o_banks[m][:, 1, :], func=FUNC.Copy, scale=factors[m][:, 1:2]
            )
            seconds[m] = second

        def combine(m):
            x = work.tile([P, PAIR_DIM], F32, name="x")
            nc.vector.scalar_tensor_tensor(
                out=x[:],
                in0=o_banks[m][:, 0, :],
                scalar=factors[m][:, 0:1],
                in1=seconds[m][:],
                op0=ALU.mult,
                op1=ALU.add,
            )
            xs[m] = x

        def measure(m):
            squares = work.tile([P, PAIR_DIM], F32, name="squares")
            sum_sq = small.tile([P, 1], F32, name="sum_sq")
            nc.scalar.activation(out=squares[:], in_=xs[m][:], func=FUNC.Square, accum_out=sum_sq[:])
            floored = small.tile([P, 1], F32, name="floored")
            nc.gpsimd.tensor_scalar_add(out=floored[:], in0=sum_sq[:], scalar1=PAIR_DIM * EPS)
            rstd = small.tile([P, 1], F32, name="rstd")
            nc.gpsimd.tensor_tensor(out=rstd[:], in0=floored[:], in1=minus_half[:], op=ALU.pow)
            rstds[m] = rstd

        def finish(m):
            i, pair = divmod(m, 2)
            y = work.tile([P, PAIR_DIM], F32, name="y")
            nc.vector.scalar_tensor_tensor(
                out=y[:],
                in0=xs[m][:],
                scalar=rstds[m][:, 0:1],
                in1=gain[:],
                op0=ALU.mult,
                op1=ALU.mult,
            )
            nc.sync.dma_start(
                out=out_rows[:, i, pair * PAIR_DIM : (pair + 1) * PAIR_DIM], in_=y[:]
            )

        def run(stage, index, count):
            if 0 <= index < count:
                stage(index)

        def run_pair(stage, n, lag):
            if (n - lag) % 2 == 0:
                run(stage, (n - lag) // 2, PAIR_UNITS)

        def tick(n):
            run_pair(scale_second, n, 5)
            run_pair(measure, n, 7)
            run(exponent, n, UNITS)
            run(regroup, n - 1, UNITS)
            if n == LAM_TICK + 1:
                lam_products()
            if n == LAM_TICK + 2:
                scale_gain()
            if n == LAM_TICK + 3:
                lam_dots()
            if n == LAM_TICK + 4:
                lam_signs()
            run(row_tops, n + 1, UNITS)
            run(quantise, n - 2, UNITS)
            run(shift, n + 1, UNITS)
            run_pair(combine, n, 5)
            run_pair(finish, n, 11)
            if n % HEADS == 1:
                run(copy_rows, n // HEADS + 2, Q_TILES)
            round_of_pass = HEADS * TILES_PER_PASS
            if (n + 1) % round_of_pass == 0:
                run(regroup_values, (n + 1) // round_of_pass, PASSES)
            if n % round_of_pass == 0:
                run(quantise_values, n // round_of_pass, PASSES)
            run_pair(weigh, n, 2)
            run(scores, n + 2, UNITS)
            run(turn, n, UNITS)
            run(attend, n - 2, UNITS)
            if n % HEADS == 0:
                run(turn_rows, n // HEADS + 2, Q_TILES)
            if n == LAM_TICK:
                spread_vectors()

        first_tick = -2 * HEADS
        last_tick = 2 * (PAIR_UNITS - 1) + 11
        with tc.manual_schedule():
            for n in range(first_tick, last_tick + 1):
                tick(n)
